import numpy as np
import ml_dtypes


def mxq(x, axis, fmt="e4m3"):
    dtype, down = {"e4m3": (ml_dtypes.float8_e4m3fn, 7), "e5m2": (ml_dtypes.float8_e5m2, 14)}[fmt]
    v = np.moveaxis(np.asarray(x, np.float32).astype(ml_dtypes.bfloat16).astype(np.float64), axis, -1)
    blocks = v.reshape(v.shape[:-1] + (-1, 32))
    amax = np.abs(blocks).max(-1, keepdims=True)
    byte = np.maximum(np.where(amax > 0, np.frexp(amax)[1] - 1 + 127, 0) - down, 1)
    scale = np.exp2(byte - 127.0)
    codes = (blocks / scale).astype(np.float32).astype(dtype).astype(np.float64)
    return np.moveaxis((codes * scale).reshape(v.shape), -1, axis)


WIDE = False


def mx_kscale(k):
    if not WIDE:
        return np.ones(k)
    levels = np.array([10, -10, 5, -5, 0])
    a = np.random.permutation(np.resize(levels, k // 512 * 4)).reshape(k // 512, 4)
    idx = np.arange(k)
    return np.exp2(a[idx // 512, idx % 128 // 32])


BF16 = ml_dtypes.bfloat16


def bf(x):
    return np.asarray(x, np.float32).astype(BF16)


def f64(x):
    return np.asarray(x).astype(np.float64)


E2M1 = np.array([0.0, 0.5, 1.0, 1.5, 2.0, 3.0, 4.0, 6.0, -0.0, -0.5, -1.0, -1.5, -2.0, -3.0, -4.0, -6.0])


def pack_weight(w, fmt):
    k, n = w.shape
    w = f64(bf(w)).reshape(k // 32, 32, n)
    amax = np.abs(w).max(1)
    if fmt == "e4m3":
        byte = np.frexp(amax)[1] - 1 + 127 - 7
    else:
        mant, ex = np.frexp(amax / 6.0)
        byte = np.where(mant > 0.5, ex, ex - 1) + 127
    byte = np.clip(np.where(amax > 0, byte, 1), 1, 254)
    scaled = (w * np.exp2(127.0 - byte)[:, None, :]).reshape(k, n).astype(np.float32)
    by_word = np.ascontiguousarray(scaled.reshape(k // 512, 128, 4, n).transpose(0, 1, 3, 2))
    if fmt == "e4m3":
        words = by_word.astype(ml_dtypes.float8_e4m3fn).view(np.uint8)
    else:
        c = by_word.astype(ml_dtypes.float4_e2m1fn).view(np.uint8) & 0xF
        words = c[..., 0::2] | (c[..., 1::2] << 4)
    return np.ascontiguousarray(words), np.ascontiguousarray(byte.astype(np.uint8).reshape(k // 512, 16, n))


def unpack_weight(words, scales, fmt):
    g, p, n, _ = words.shape
    if fmt == "e4m3":
        vals = np.ascontiguousarray(words).view(ml_dtypes.float8_e4m3fn).astype(np.float64)
    else:
        nib = np.empty((g, p, n, 4), np.uint8)
        nib[..., 0::2] = words & 0xF
        nib[..., 1::2] = words >> 4
        vals = E2M1[nib]
    vals = vals * np.repeat(np.exp2(scales.astype(np.float64) - 127.0), 8, axis=1)[..., None]
    return vals.transpose(0, 1, 3, 2).reshape(g * 512, n)


B, N, F, G, K = 4, 512, 512, 512, 2048
EPS = 1e-8


def setup_inputs():
    s = mx_kscale(F)
    a = np.random.standard_normal((B, N, 1))
    g = np.random.standard_normal((B, 1, F))
    h = 2.0 * (np.random.standard_normal((B, N, F)) + a * g)
    w = (np.random.standard_normal((F, G)) + 0.5 * np.random.standard_normal((F, 1))) / np.sqrt(F)
    words, scales = pack_weight(w / s[:, None], "e4m3")
    return {"h": bf(h * s), "W_h_words": words, "W_h_scales": scales, "beta": bf(2.0 + np.random.uniform(size=1))}


def reference(h, W_h_words, W_h_scales, beta):
    Wh = mxq(f64(h), 2, "e4m3") @ unpack_weight(W_h_words, W_h_scales, "e4m3")
    xm = Wh - Wh.mean(-1, keepdims=True)
    xq = mxq(xm, 2, "e4m3")
    cov = xq @ xq.transpose(0, 2, 1)
    norm = np.sqrt((xm * xm).sum(-1))
    denom = norm[:, :, None] * norm[:, None, :] + EPS
    return f64(beta) * np.abs(cov / denom)

@@ -1,0 +1,212 @@
+import concourse.mybir as mybir
+from concourse.masks import make_identity
+
+F32 = mybir.dt.float32
+BF16 = mybir.dt.bfloat16
+I32 = mybir.dt.int32
+U32 = mybir.dt.uint32
+U8 = mybir.dt.uint8
+FP8X4 = mybir.dt.float8_e4m3fn_x4
+ACT = mybir.ActivationFunctionType
+ALU = mybir.AluOpType
+
+P = 128
+PACK = 4
+GRAPHS = 4
+NODES = 512
+FEATURES = 512
+TILES = NODES // P
+WORD_HALVES = 2
+EPS = 1e-8
+TINY = 1e-30
+
+FLOPS = 2 * GRAPHS * NODES * FEATURES * FEATURES + 2 * GRAPHS * NODES * NODES * FEATURES
+
+
+def block(i):
+    return slice(i * P, (i + 1) * P)
+
+
+def tile_pearsonattention_pa_kernel(tc, h, W_h_words, W_h_scales, beta, out):
+    nc = tc.nc
+    with (
+        tc.tile_pool(name="const", bufs=1) as const,
+        tc.tile_pool(name="inputs", bufs=GRAPHS) as inputs,
+        tc.tile_pool(name="stage", bufs=2) as stage,
+        tc.tile_pool(name="quantised", bufs=2) as quantised,
+        tc.tile_pool(name="small", bufs=2) as small,
+        tc.tile_pool(name="work", bufs=4) as work,
+        tc.psum_pool(name="psum", bufs=2) as psum,
+    ):
+        one = const.tile([P, 1], F32)
+        nc.vector.memset(one[:], 1.0)
+        table_warm = const.tile([P, 1], F32)
+        nc.scalar.activation(out=table_warm[:], in_=one[:], func=ACT.Abs_reciprocal_sqrt)
+
+        identity = const.tile([P, P], F32)
+        make_identity(nc, identity[:])
+
+        w_scales = const.tile([P, FEATURES], U8, align_bytes=64)
+        nc.vector.memset(w_scales[:].bitcast(I32), 0)
+
+        h_rows = []
+        for b in range(GRAPHS):
+            h_rows.append(inputs.tile([P, TILES, FEATURES], BF16, name="h_rows"))
+
+        def load_h(b):
+            nc.sync.dma_start(out=h_rows[b][:], in_=h[b].rearrange("(j p) f -> p j f", p=P))
+
+        load_h(0)
+        scale_rows = W_h_scales[0].bitcast(I32)
+        for quadrant in range(4):
+            nc.sync.dma_start(
+                out=w_scales[32 * quadrant : 32 * quadrant + 4, :].bitcast(I32),
+                in_=scale_rows[4 * quadrant : 4 * quadrant + 4, :],
+            )
+        w_codes = const.tile([P, FEATURES], U32, align_bytes=64)
+        nc.sync.dma_start(out=w_codes[:].bitcast(I32), in_=W_h_words[0].rearrange("p n t -> p (n t)").bitcast(I32))
+        for b in range(1, GRAPHS):
+            load_h(b)
+
+        beta_bf16 = const.tile([P, 1], BF16)
+        nc.scalar.dma_start(out=beta_bf16[:], in_=beta.partition_broadcast(P))
+        beta_f32 = const.tile([P, 1], F32)
+        nc.vector.tensor_copy(out=beta_f32[:], in_=beta_bf16[:])
+
+        for b in range(GRAPHS):
+            h_grouped = stage.tile([P, NODES, PACK], BF16, align_bytes=64)
+            h_grouped_words = (
+                h_grouped[:]
+                .rearrange("p r t -> p (r t)")
+                .bitcast(F32)
+                .rearrange("p (j r u) -> p j r u", j=TILES, u=WORD_HALVES)
+            )
+            for pair in range(TILES // 2):
+                hT_ps = psum.tile([P, 2, WORD_HALVES, P], F32, tag="transposed")
+                for jj in range(2):
+                    words = h_rows[b][:, 2 * pair + jj, :].bitcast(F32)
+                    for u in range(WORD_HALVES):
+                        nc.tensor.transpose(
+                            out=hT_ps[:, jj, u, :],
+                            in_=words[:, u : FEATURES // 2 : WORD_HALVES],
+                            identity=identity[:],
+                        )
+                nc.scalar.copy(
+                    out=h_grouped_words[:, 2 * pair : 2 * pair + 2, :, :],
+                    in_=hT_ps[:].rearrange("p j u r -> p j r u"),
+                )
+            hq_codes = quantised.tile([P, NODES], U32, align_bytes=64)
+            hq_scales = quantised.tile([P, NODES], U8, align_bytes=64)
+            nc.vector.quantize_mx(
+                out=hq_codes[:].bitcast(FP8X4),
+                scales=hq_scales[:],
+                in_=h_grouped[:].rearrange("p r t -> p (r t)"),
+            )
+
+            stats = small.tile([P, TILES, 6], F32)
+            mean_var = small.tile([P, TILES, 2], F32)
+            for j in range(TILES):
+                wh_ps = psum.tile([P, FEATURES], F32)
+                nc.tensor.matmul_mx(
+                    out=wh_ps[:],
+                    lhsT=hq_codes[:, block(j)].bitcast(FP8X4),
+                    lhsT_scale=hq_scales[:, block(j)],
+                    rhs=w_codes[:].bitcast(FP8X4),
+                    rhs_scale=w_scales[:],
+                    start=True,
+                    stop=True,
+                )
+                nc.vector.bn_stats(out=stats[:, j, :], in_=wh_ps[:])
+            for j in range(TILES):
+                nc.vector.bn_aggr(out=mean_var[:, j, :], in_=stats[:, j, :])
+
+            sum_squares = small.tile([P, TILES], F32)
+            nc.vector.tensor_scalar(
+                out=sum_squares[:],
+                in0=mean_var[:, :, 1],
+                scalar1=float(FEATURES),
+                scalar2=TINY,
+                op0=ALU.mult,
+                op1=ALU.max,
+            )
+            inv_norm = small.tile([P, TILES], F32)
+            nc.scalar.activation(out=inv_norm[:], in_=sum_squares[:], func=ACT.Abs_reciprocal_sqrt)
+            norm = small.tile([P, TILES], F32)
+            nc.vector.reciprocal(out=norm[:], in_=inv_norm[:])
+
+            mean_ps = psum.tile([P, NODES], F32, tag="transposed")
+            for j in range(TILES):
+                nc.tensor.transpose(
+                    out=mean_ps[:, block(j)], in_=mean_var[:, j, 0:1].to_broadcast([P, P]), identity=identity[:]
+                )
+            mean_rows = stage.tile([P, NODES], F32)
+            nc.scalar.copy(out=mean_rows[:], in_=mean_ps[:])
+            norm_ps = psum.tile([P, NODES], F32, tag="transposed")
+            for j in range(TILES):
+                nc.tensor.transpose(
+                    out=norm_ps[:, block(j)], in_=norm[:, j : j + 1].to_broadcast([P, P]), identity=identity[:]
+                )
+            norm_rows = stage.tile([P, NODES], F32)
+            nc.scalar.copy(out=norm_rows[:], in_=norm_ps[:])
+
+            x_grouped = stage.tile([P, NODES, PACK], BF16, align_bytes=64)
+            for j in range(TILES):
+                whT_ps = psum.tile([P, PACK, P], F32)
+                for t in range(PACK):
+                    nc.tensor.matmul_mx(
+                        out=whT_ps[:, t, :],
+                        lhsT=w_codes[:, block(t)].bitcast(FP8X4),
+                        lhsT_scale=w_scales[:, block(t)],
+                        rhs=hq_codes[:, block(j)].bitcast(FP8X4),
+                        rhs_scale=hq_scales[:, block(j)],
+                        start=True,
+                        stop=True,
+                    )
+                nc.vector.tensor_tensor(
+                    out=x_grouped[:, block(j), :],
+                    in0=whT_ps[:].rearrange("p t r -> p r t"),
+                    in1=mean_rows[:, block(j)].unsqueeze(2).to_broadcast([P, P, PACK]),
+                    op=ALU.subtract,
+                )
+            xq_codes = quantised.tile([P, NODES], U32, align_bytes=64)
+            xq_scales = quantised.tile([P, NODES], U8, align_bytes=64)
+            nc.vector.quantize_mx(
+                out=xq_codes[:].bitcast(FP8X4),
+                scales=xq_scales[:],
+                in_=x_grouped[:].rearrange("p r t -> p (r t)"),
+            )
+
+            for i in range(TILES):
+                rsqrt_den = work.tile([P, NODES], F32)
+                nc.scalar.activation(
+                    out=rsqrt_den[:],
+                    in_=norm_rows[:],
+                    func=ACT.Abs_reciprocal_sqrt,
+                    scale=norm[:, i : i + 1],
+                    bias=EPS,
+                )
+                inv_den = work.tile([P, NODES], F32)
+                nc.scalar.activation(out=inv_den[:], in_=rsqrt_den[:], func=ACT.Square)
+
+                cov_ps = psum.tile([P, NODES], F32)
+                nc.tensor.matmul_mx(
+                    out=cov_ps[:],
+                    lhsT=xq_codes[:, block(i)].bitcast(FP8X4),
+                    lhsT_scale=xq_scales[:, block(i)],
+                    rhs=xq_codes[:].bitcast(FP8X4),
+                    rhs_scale=xq_scales[:],
+                    start=True,
+                    stop=True,
+                )
+                abs_cov = work.tile([P, NODES], F32)
+                nc.scalar.activation(out=abs_cov[:], in_=cov_ps[:], func=ACT.Abs)
+                result = work.tile([P, NODES], F32)
+                nc.vector.scalar_tensor_tensor(
+                    out=result[:],
+                    in0=abs_cov[:],
+                    scalar=beta_f32[:, 0:1],
+                    in1=inv_den[:],
+                    op0=ALU.mult,
+                    op1=ALU.mult,
+                )
+                nc.sync.dma_start(out=out[b, block(i), :], in_=result[:])

@@ -16,7 +16,10 @@ GRAPHS = 4
 NODES = 512
 FEATURES = 512
 TILES = NODES // P
+PAIRS = TILES // 2
 WORD_HALVES = 2
+BANKS = 8
+MX_WIDTHS = (128, 256, 512)
 EPS = 1e-8
 TINY = 1e-30
 
@@ -27,17 +30,25 @@ def block(i):
     return slice(i * P, (i + 1) * P)
 
 
+def from_diagonal(i):
+    return slice(i * P, NODES)
+
+
 def tile_pearsonattention_pa_kernel(tc, h, W_h_words, W_h_scales, beta, out):
     nc = tc.nc
     with (
         tc.tile_pool(name="const", bufs=1) as const,
-        tc.tile_pool(name="inputs", bufs=GRAPHS) as inputs,
-        tc.tile_pool(name="stage", bufs=2) as stage,
-        tc.tile_pool(name="quantised", bufs=2) as quantised,
-        tc.tile_pool(name="small", bufs=2) as small,
-        tc.tile_pool(name="work", bufs=4) as work,
-        tc.psum_pool(name="psum", bufs=2) as psum,
+        tc.tile_pool(name="every_graph", bufs=GRAPHS) as every_graph,
+        tc.tile_pool(name="two_graphs", bufs=2) as two_graphs,
+        tc.tile_pool(name="two_graphs_row_tiles", bufs=2 * TILES) as row_tiles,
+        tc.psum_pool(name="psum", bufs=BANKS) as psum,
+        tc.manual_schedule(),
     ):
+        def bank():
+            return psum.tile([P, NODES], F32, name="bank")
+
+        tiles = {}
+
         one = const.tile([P, 1], F32)
         nc.vector.memset(one[:], 1.0)
         table_warm = const.tile([P, 1], F32)
@@ -49,12 +60,13 @@ def tile_pearsonattention_pa_kernel(tc, h, W_h_words, W_h_scales, beta, out):
         w_scales = const.tile([P, FEATURES], U8, align_bytes=64)
         nc.vector.memset(w_scales[:].bitcast(I32), 0)
 
-        h_rows = []
-        for b in range(GRAPHS):
-            h_rows.append(inputs.tile([P, TILES, FEATURES], BF16, name="h_rows"))
-
         def load_h(b):
-            nc.sync.dma_start(out=h_rows[b][:], in_=h[b].rearrange("(j p) f -> p j f", p=P))
+            h_rows = every_graph.tile([P, TILES, FEATURES], BF16, name="h_rows")
+            tiles["h_rows", b] = h_rows
+            rows = h[b].rearrange("(j p) f -> p j f", p=P)
+            for pair in range(PAIRS):
+                two = slice(2 * pair, 2 * pair + 2)
+                nc.sync.dma_start(out=h_rows[:, two, :], in_=rows[:, two, :])
 
         load_h(0)
         scale_rows = W_h_scales[0].bitcast(I32)
@@ -73,140 +85,252 @@ def tile_pearsonattention_pa_kernel(tc, h, W_h_words, W_h_scales, beta, out):
         beta_f32 = const.tile([P, 1], F32)
         nc.vector.tensor_copy(out=beta_f32[:], in_=beta_bf16[:])
 
-        for b in range(GRAPHS):
-            h_grouped = stage.tile([P, NODES, PACK], BF16, align_bytes=64)
-            h_grouped_words = (
-                h_grouped[:]
+        def transpose_h(b, pair):
+            if pair == 0:
+                tiles["h_grouped", b] = every_graph.tile([P, NODES, PACK], BF16, align_bytes=64, name="h_grouped")
+            hT = bank()[:].rearrange("p (j u r) -> p j u r", j=2, u=WORD_HALVES)
+            for jj in range(2):
+                words = tiles["h_rows", b][:, 2 * pair + jj, :].bitcast(F32)
+                for u in range(WORD_HALVES):
+                    nc.tensor.transpose(
+                        out=hT[:, jj, u, :], in_=words[:, u : FEATURES // 2 : WORD_HALVES], identity=identity[:]
+                    )
+            grouped_words = (
+                tiles["h_grouped", b][:]
                 .rearrange("p r t -> p (r t)")
                 .bitcast(F32)
                 .rearrange("p (j r u) -> p j r u", j=TILES, u=WORD_HALVES)
             )
-            for pair in range(TILES // 2):
-                hT_ps = psum.tile([P, 2, WORD_HALVES, P], F32, tag="transposed")
-                for jj in range(2):
-                    words = h_rows[b][:, 2 * pair + jj, :].bitcast(F32)
-                    for u in range(WORD_HALVES):
-                        nc.tensor.transpose(
-                            out=hT_ps[:, jj, u, :],
-                            in_=words[:, u : FEATURES // 2 : WORD_HALVES],
-                            identity=identity[:],
-                        )
-                nc.scalar.copy(
-                    out=h_grouped_words[:, 2 * pair : 2 * pair + 2, :, :],
-                    in_=hT_ps[:].rearrange("p j u r -> p j r u"),
-                )
-            hq_codes = quantised.tile([P, NODES], U32, align_bytes=64)
-            hq_scales = quantised.tile([P, NODES], U8, align_bytes=64)
-            nc.vector.quantize_mx(
-                out=hq_codes[:].bitcast(FP8X4),
-                scales=hq_scales[:],
-                in_=h_grouped[:].rearrange("p r t -> p (r t)"),
+            nc.scalar.copy(
+                out=grouped_words[:, 2 * pair : 2 * pair + 2, :, :], in_=hT.rearrange("p j u r -> p j r u")
             )
 
-            stats = small.tile([P, TILES, 6], F32)
-            mean_var = small.tile([P, TILES, 2], F32)
-            for j in range(TILES):
-                wh_ps = psum.tile([P, FEATURES], F32)
+        def quantise(b, grouped, codes, scales, nodes):
+            if (codes, b) not in tiles:
+                tiles[codes, b] = two_graphs.tile([P, NODES], U32, align_bytes=64, name=codes)
+                tiles[scales, b] = two_graphs.tile([P, NODES], U8, align_bytes=64, name=scales)
+            nc.vector.quantize_mx(
+                out=tiles[codes, b][:, nodes].bitcast(FP8X4),
+                scales=tiles[scales, b][:, nodes],
+                in_=tiles[grouped, b][:, nodes, :].rearrange("p r t -> p (r t)"),
+            )
+
+        def quantise_h(b, pair):
+            quantise(b, "h_grouped", "hq_codes", "hq_scales", slice(2 * pair * P, 2 * (pair + 1) * P))
+
+        def quantise_x(b):
+            quantise(b, "x_grouped", "xq_codes", "xq_scales", slice(0, NODES))
+
+        def node_statistics(b, j):
+            if j == 0:
+                tiles["stats", b] = two_graphs.tile([P, TILES, 6], F32, name="stats")
+            wh = bank()
+            nc.tensor.matmul_mx(
+                out=wh[:],
+                lhsT=tiles["hq_codes", b][:, block(j)].bitcast(FP8X4),
+                lhsT_scale=tiles["hq_scales", b][:, block(j)],
+                rhs=w_codes[:].bitcast(FP8X4),
+                rhs_scale=w_scales[:],
+                start=True,
+                stop=True,
+            )
+            nc.vector.bn_stats(out=tiles["stats", b][:, j, :], in_=wh[:])
+
+        def project_features(b, j):
+            whT = bank()
+            tiles["whT", b, j] = whT
+            for t in range(PACK):
                 nc.tensor.matmul_mx(
-                    out=wh_ps[:],
-                    lhsT=hq_codes[:, block(j)].bitcast(FP8X4),
-                    lhsT_scale=hq_scales[:, block(j)],
-                    rhs=w_codes[:].bitcast(FP8X4),
-                    rhs_scale=w_scales[:],
+                    out=whT[:, block(t)],
+                    lhsT=w_codes[:, block(t)].bitcast(FP8X4),
+                    lhsT_scale=w_scales[:, block(t)],
+                    rhs=tiles["hq_codes", b][:, block(j)].bitcast(FP8X4),
+                    rhs_scale=tiles["hq_scales", b][:, block(j)],
                     start=True,
                     stop=True,
                 )
-                nc.vector.bn_stats(out=stats[:, j, :], in_=wh_ps[:])
-            for j in range(TILES):
-                nc.vector.bn_aggr(out=mean_var[:, j, :], in_=stats[:, j, :])
 
-            sum_squares = small.tile([P, TILES], F32)
+        def mean_and_variance(b, j):
+            if j == 0:
+                tiles["mean_var", b] = two_graphs.tile([P, TILES, 2], F32, name="mean_var")
+            nc.vector.bn_aggr(out=tiles["mean_var", b][:, j, :], in_=tiles["stats", b][:, j, :])
+
+        def inverse_norm(b):
+            sum_squares = two_graphs.tile([P, TILES], F32, name="sum_squares")
             nc.vector.tensor_scalar(
                 out=sum_squares[:],
-                in0=mean_var[:, :, 1],
+                in0=tiles["mean_var", b][:, :, 1],
                 scalar1=float(FEATURES),
                 scalar2=TINY,
                 op0=ALU.mult,
                 op1=ALU.max,
             )
-            inv_norm = small.tile([P, TILES], F32)
-            nc.scalar.activation(out=inv_norm[:], in_=sum_squares[:], func=ACT.Abs_reciprocal_sqrt)
-            norm = small.tile([P, TILES], F32)
-            nc.vector.reciprocal(out=norm[:], in_=inv_norm[:])
+            tiles["inv_norm", b] = two_graphs.tile([P, TILES], F32, name="inv_norm")
+            nc.scalar.activation(out=tiles["inv_norm", b][:], in_=sum_squares[:], func=ACT.Abs_reciprocal_sqrt)
 
-            mean_ps = psum.tile([P, NODES], F32, tag="transposed")
-            for j in range(TILES):
-                nc.tensor.transpose(
-                    out=mean_ps[:, block(j)], in_=mean_var[:, j, 0:1].to_broadcast([P, P]), identity=identity[:]
-                )
-            mean_rows = stage.tile([P, NODES], F32)
-            nc.scalar.copy(out=mean_rows[:], in_=mean_ps[:])
-            norm_ps = psum.tile([P, NODES], F32, tag="transposed")
-            for j in range(TILES):
-                nc.tensor.transpose(
-                    out=norm_ps[:, block(j)], in_=norm[:, j : j + 1].to_broadcast([P, P]), identity=identity[:]
-                )
-            norm_rows = stage.tile([P, NODES], F32)
-            nc.scalar.copy(out=norm_rows[:], in_=norm_ps[:])
+        def norm_from_inverse(b):
+            tiles["norm", b] = two_graphs.tile([P, TILES], F32, name="norm")
+            nc.vector.reciprocal(out=tiles["norm", b][:], in_=tiles["inv_norm", b][:])
 
-            x_grouped = stage.tile([P, NODES, PACK], BF16, align_bytes=64)
-            for j in range(TILES):
-                whT_ps = psum.tile([P, PACK, P], F32)
-                for t in range(PACK):
-                    nc.tensor.matmul_mx(
-                        out=whT_ps[:, t, :],
-                        lhsT=w_codes[:, block(t)].bitcast(FP8X4),
-                        lhsT_scale=w_scales[:, block(t)],
-                        rhs=hq_codes[:, block(j)].bitcast(FP8X4),
-                        rhs_scale=hq_scales[:, block(j)],
-                        start=True,
-                        stop=True,
-                    )
-                nc.vector.tensor_tensor(
-                    out=x_grouped[:, block(j), :],
-                    in0=whT_ps[:].rearrange("p t r -> p r t"),
-                    in1=mean_rows[:, block(j)].unsqueeze(2).to_broadcast([P, P, PACK]),
-                    op=ALU.subtract,
+        def spread(b, column_of_tile, rows, first, count):
+            if (rows, b) not in tiles:
+                tiles[rows, b] = two_graphs.tile([P, NODES], F32, name=rows)
+            spread_ps = bank()
+            for j in range(first, first + count):
+                nc.tensor.transpose(
+                    out=spread_ps[:, block(j)], in_=column_of_tile(j).to_broadcast([P, P]), identity=identity[:]
                 )
-            xq_codes = quantised.tile([P, NODES], U32, align_bytes=64)
-            xq_scales = quantised.tile([P, NODES], U8, align_bytes=64)
-            nc.vector.quantize_mx(
-                out=xq_codes[:].bitcast(FP8X4),
-                scales=xq_scales[:],
-                in_=x_grouped[:].rearrange("p r t -> p (r t)"),
+            nodes = slice(first * P, (first + count) * P)
+            nc.scalar.copy(out=tiles[rows, b][:, nodes], in_=spread_ps[:, nodes])
+
+        def spread_mean(b, pair):
+            spread(b, lambda j: tiles["mean_var", b][:, j, 0:1], "mean_rows", 2 * pair, 2)
+
+        def spread_norm(b):
+            spread(b, lambda j: tiles["norm", b][:, j : j + 1], "norm_rows", 0, TILES)
+
+        def subtract_mean(b, j):
+            if j == 0:
+                tiles["x_grouped", b] = two_graphs.tile([P, NODES, PACK], BF16, align_bytes=64, name="x_grouped")
+            nc.vector.tensor_tensor(
+                out=tiles["x_grouped", b][:, block(j), :],
+                in0=tiles["whT", b, j][:].rearrange("p (t r) -> p r t", t=PACK),
+                in1=tiles["mean_rows", b][:, block(j)].unsqueeze(2).to_broadcast([P, P, PACK]),
+                op=ALU.subtract,
             )
 
-            for i in range(TILES):
-                rsqrt_den = work.tile([P, NODES], F32)
-                nc.scalar.activation(
-                    out=rsqrt_den[:],
-                    in_=norm_rows[:],
-                    func=ACT.Abs_reciprocal_sqrt,
-                    scale=norm[:, i : i + 1],
-                    bias=EPS,
-                )
-                inv_den = work.tile([P, NODES], F32)
-                nc.scalar.activation(out=inv_den[:], in_=rsqrt_den[:], func=ACT.Square)
+        def inverse_denominator(b, i):
+            own = from_diagonal(i)
+            rsqrt_den = row_tiles.tile([P, NODES], F32, name="rsqrt_den")
+            nc.scalar.activation(
+                out=rsqrt_den[:, own],
+                in_=tiles["norm_rows", b][:, own],
+                func=ACT.Abs_reciprocal_sqrt,
+                scale=tiles["norm", b][:, i : i + 1],
+                bias=EPS,
+            )
+            tiles["inv_den", b, i] = row_tiles.tile([P, NODES], F32, name="inv_den")
+            nc.scalar.activation(out=tiles["inv_den", b, i][:, own], in_=rsqrt_den[:, own], func=ACT.Square)
 
-                cov_ps = psum.tile([P, NODES], F32)
-                nc.tensor.matmul_mx(
-                    out=cov_ps[:],
-                    lhsT=xq_codes[:, block(i)].bitcast(FP8X4),
-                    lhsT_scale=xq_scales[:, block(i)],
-                    rhs=xq_codes[:].bitcast(FP8X4),
-                    rhs_scale=xq_scales[:],
-                    start=True,
-                    stop=True,
-                )
-                abs_cov = work.tile([P, NODES], F32)
-                nc.scalar.activation(out=abs_cov[:], in_=cov_ps[:], func=ACT.Abs)
-                result = work.tile([P, NODES], F32)
-                nc.vector.scalar_tensor_tensor(
-                    out=result[:],
-                    in0=abs_cov[:],
-                    scalar=beta_f32[:, 0:1],
-                    in1=inv_den[:],
-                    op0=ALU.mult,
-                    op1=ALU.mult,
-                )
-                nc.sync.dma_start(out=out[b, block(i), :], in_=result[:])
+        def covariance(b, i):
+            width = min(w for w in MX_WIDTHS if w >= NODES - i * P)
+            columns = slice(NODES - width, NODES)
+            cov = bank()
+            tiles["cov", b, i] = cov
+            nc.tensor.matmul_mx(
+                out=cov[:, columns],
+                lhsT=tiles["xq_codes", b][:, block(i)].bitcast(FP8X4),
+                lhsT_scale=tiles["xq_scales", b][:, block(i)],
+                rhs=tiles["xq_codes", b][:, columns].bitcast(FP8X4),
+                rhs_scale=tiles["xq_scales", b][:, columns],
+                start=True,
+                stop=True,
+            )
+
+        def absolute(b, i):
+            own = from_diagonal(i)
+            tiles["abs_cov", b, i] = row_tiles.tile([P, NODES], F32, name="abs_cov")
+            nc.scalar.activation(out=tiles["abs_cov", b, i][:, own], in_=tiles["cov", b, i][:, own], func=ACT.Abs)
+
+        def scale_own_columns(b, i):
+            own = from_diagonal(i)
+            tiles["result", b, i] = row_tiles.tile([P, NODES], F32, name="result")
+            nc.vector.scalar_tensor_tensor(
+                out=tiles["result", b, i][:, own],
+                in0=tiles["abs_cov", b, i][:, own],
+                scalar=beta_f32[:, 0:1],
+                in1=tiles["inv_den", b, i][:, own],
+                op0=ALU.mult,
+                op1=ALU.mult,
+            )
+
+        def mirror_and_store(b, i):
+            if i > 0:
+                mirrored = bank()
+                for j in range(i):
+                    nc.tensor.transpose(
+                        out=mirrored[:, block(j)], in_=tiles["result", b, j][:, block(i)], identity=identity[:]
+                    )
+                nc.scalar.copy(out=tiles["result", b, i][:, 0 : i * P], in_=mirrored[:, 0 : i * P])
+            nc.sync.dma_start(out=out[b, block(i), :], in_=tiles["result", b, i][:])
+
+        def statistics_of_graph(b, between):
+            node_statistics(b, 0)
+            node_statistics(b, 1)
+            between(0)
+            mean_and_variance(b, 0)
+            node_statistics(b, 2)
+            between(1)
+            mean_and_variance(b, 1)
+            node_statistics(b, 3)
+            mean_and_variance(b, 2)
+            mean_and_variance(b, 3)
+
+        for pair in range(PAIRS):
+            transpose_h(0, pair)
+            quantise_h(0, pair)
+        statistics_of_graph(0, lambda k: transpose_h(1, k))
+        for j in range(TILES):
+            project_features(0, j)
+        inverse_norm(0)
+        for pair in range(PAIRS):
+            spread_mean(0, pair)
+        for pair in range(PAIRS):
+            transpose_h(2, pair)
+        subtract_mean(0, 0)
+        subtract_mean(0, 1)
+        norm_from_inverse(0)
+        spread_norm(0)
+        subtract_mean(0, 2)
+        for pair in range(PAIRS):
+            quantise_h(1, pair)
+        subtract_mean(0, 3)
+        for i in range(TILES):
+            inverse_denominator(0, i)
+
+        for b in range(GRAPHS):
+            nxt = b + 1
+            more = nxt < GRAPHS
+            quantise_x(b)
+            if more:
+                statistics_of_graph(nxt, lambda k: covariance(b, k))
+            else:
+                covariance(b, 0)
+                covariance(b, 1)
+            absolute(b, 0)
+            absolute(b, 1)
+            covariance(b, 2)
+            covariance(b, 3)
+            if more:
+                for j in range(TILES):
+                    project_features(nxt, j)
+            absolute(b, 2)
+            absolute(b, 3)
+            if more:
+                inverse_norm(nxt)
+                for pair in range(PAIRS):
+                    spread_mean(nxt, pair)
+            scale_own_columns(b, 0)
+            mirror_and_store(b, 0)
+            scale_own_columns(b, 1)
+            if more:
+                norm_from_inverse(nxt)
+                spread_norm(nxt)
+            scale_own_columns(b, 2)
+            scale_own_columns(b, 3)
+            if more:
+                for j in range(TILES - 1):
+                    subtract_mean(nxt, j)
+                if nxt + 1 < GRAPHS:
+                    for pair in range(PAIRS):
+                        quantise_h(nxt + 1, pair)
+                subtract_mean(nxt, TILES - 1)
+            if b + 3 < GRAPHS:
+                for pair in range(PAIRS):
+                    transpose_h(b + 3, pair)
+            for i in range(1, TILES):
+                if more:
+                    inverse_denominator(nxt, i - 1)
+                mirror_and_store(b, i)
+            if more:
+                inverse_denominator(nxt, TILES - 1)

@@ -42,7 +42,6 @@ def tile_pearsonattention_pa_kernel(tc, h, W_h_words, W_h_scales, beta, out):
         tc.tile_pool(name="two_graphs", bufs=2) as two_graphs,
         tc.tile_pool(name="two_graphs_row_tiles", bufs=2 * TILES) as row_tiles,
         tc.psum_pool(name="psum", bufs=BANKS) as psum,
-        tc.manual_schedule(),
     ):
         def bank():
             return psum.tile([P, NODES], F32, name="bank")

@@ -186,7 +186,13 @@ def tile_pearsonattention_pa_kernel(tc, h, W_h_words, W_h_scales, beta, out):
             spread(b, lambda j: tiles["mean_var", b][:, j, 0:1], "mean_rows", 2 * pair, 2)
 
         def spread_norm(b):
-            spread(b, lambda j: tiles["norm", b][:, j : j + 1], "norm_rows", 0, TILES)
+            tiles["norm_rows", b] = bank()
+            for j in range(TILES):
+                nc.tensor.transpose(
+                    out=tiles["norm_rows", b][:, block(j)],
+                    in_=tiles["norm", b][:, j : j + 1].to_broadcast([P, P]),
+                    identity=identity[:],
+                )
 
         def subtract_mean(b, j):
             if j == 0:
@@ -198,18 +204,32 @@ def tile_pearsonattention_pa_kernel(tc, h, W_h_words, W_h_scales, beta, out):
                 op=ALU.subtract,
             )
 
-        def inverse_denominator(b, i):
+        def rsqrt_denominator(b, i):
             own = from_diagonal(i)
-            rsqrt_den = row_tiles.tile([P, NODES], F32, name="rsqrt_den")
+            tiles["rsqrt_den", b, i] = row_tiles.tile([P, NODES], F32, name="rsqrt_den")
             nc.scalar.activation(
-                out=rsqrt_den[:, own],
+                out=tiles["rsqrt_den", b, i][:, own],
                 in_=tiles["norm_rows", b][:, own],
                 func=ACT.Abs_reciprocal_sqrt,
                 scale=tiles["norm", b][:, i : i + 1],
                 bias=EPS,
             )
+
+        def square_denominator(b, i):
+            own = from_diagonal(i)
             tiles["inv_den", b, i] = row_tiles.tile([P, NODES], F32, name="inv_den")
-            nc.scalar.activation(out=tiles["inv_den", b, i][:, own], in_=rsqrt_den[:, own], func=ACT.Square)
+            nc.scalar.activation(
+                out=tiles["inv_den", b, i][:, own], in_=tiles["rsqrt_den", b, i][:, own], func=ACT.Square
+            )
+
+        def inverse_denominators(b, between):
+            rsqrt_denominator(b, 0)
+            rsqrt_denominator(b, 1)
+            for i in range(TILES):
+                between(i)
+                square_denominator(b, i)
+                if i + 2 < TILES:
+                    rsqrt_denominator(b, i + 2)
 
         def covariance(b, i):
             width = min(w for w in MX_WIDTHS if w >= NODES - i * P)
@@ -243,14 +263,18 @@ def tile_pearsonattention_pa_kernel(tc, h, W_h_words, W_h_scales, beta, out):
                 op1=ALU.mult,
             )
 
-        def mirror_and_store(b, i):
+        def mirror(b, i):
+            tiles["mirrored", b, i] = bank()
+            for j in range(i):
+                nc.tensor.transpose(
+                    out=tiles["mirrored", b, i][:, block(j)],
+                    in_=tiles["result", b, j][:, block(i)],
+                    identity=identity[:],
+                )
+
+        def complete_and_store(b, i):
             if i > 0:
-                mirrored = bank()
-                for j in range(i):
-                    nc.tensor.transpose(
-                        out=mirrored[:, block(j)], in_=tiles["result", b, j][:, block(i)], identity=identity[:]
-                    )
-                nc.scalar.copy(out=tiles["result", b, i][:, 0 : i * P], in_=mirrored[:, 0 : i * P])
+                nc.scalar.copy(out=tiles["result", b, i][:, 0 : i * P], in_=tiles["mirrored", b, i][:, 0 : i * P])
             nc.sync.dma_start(out=out[b, block(i), :], in_=tiles["result", b, i][:])
 
         def statistics_of_graph(b, between):
@@ -271,21 +295,18 @@ def tile_pearsonattention_pa_kernel(tc, h, W_h_words, W_h_scales, beta, out):
         statistics_of_graph(0, lambda k: transpose_h(1, k))
         for j in range(TILES):
             project_features(0, j)
+        for pair in range(PAIRS):
+            quantise_h(1, pair)
         inverse_norm(0)
         for pair in range(PAIRS):
             spread_mean(0, pair)
         for pair in range(PAIRS):
             transpose_h(2, pair)
-        subtract_mean(0, 0)
-        subtract_mean(0, 1)
+        for j in range(TILES):
+            subtract_mean(0, j)
         norm_from_inverse(0)
         spread_norm(0)
-        subtract_mean(0, 2)
-        for pair in range(PAIRS):
-            quantise_h(1, pair)
-        subtract_mean(0, 3)
-        for i in range(TILES):
-            inverse_denominator(0, i)
+        inverse_denominators(0, lambda i: None)
 
         for b in range(GRAPHS):
             nxt = b + 1
@@ -305,18 +326,17 @@ def tile_pearsonattention_pa_kernel(tc, h, W_h_words, W_h_scales, beta, out):
                     project_features(nxt, j)
             absolute(b, 2)
             absolute(b, 3)
+            scale_own_columns(b, 0)
+            complete_and_store(b, 0)
             if more:
                 inverse_norm(nxt)
                 for pair in range(PAIRS):
                     spread_mean(nxt, pair)
-            scale_own_columns(b, 0)
-            mirror_and_store(b, 0)
             scale_own_columns(b, 1)
             if more:
                 norm_from_inverse(nxt)
                 spread_norm(nxt)
             scale_own_columns(b, 2)
-            scale_own_columns(b, 3)
             if more:
                 for j in range(TILES - 1):
                     subtract_mean(nxt, j)
@@ -324,12 +344,14 @@ def tile_pearsonattention_pa_kernel(tc, h, W_h_words, W_h_scales, beta, out):
                     for pair in range(PAIRS):
                         quantise_h(nxt + 1, pair)
                 subtract_mean(nxt, TILES - 1)
+            scale_own_columns(b, 3)
+            for i in range(1, TILES):
+                mirror(b, i)
             if b + 3 < GRAPHS:
                 for pair in range(PAIRS):
                     transpose_h(b + 3, pair)
-            for i in range(1, TILES):
-                if more:
-                    inverse_denominator(nxt, i - 1)
-                mirror_and_store(b, i)
             if more:
-                inverse_denominator(nxt, TILES - 1)
+                inverse_denominators(nxt, lambda i: complete_and_store(b, i + 1) if i + 1 < TILES else None)
+            else:
+                for i in range(1, TILES):
+                    complete_and_store(b, i)

@@ -155,17 +155,14 @@ def tile_pearsonattention_pa_kernel(tc, h, W_h_words, W_h_scales, beta, out):
             nc.vector.bn_aggr(out=tiles["mean_var", b][:, j, :], in_=tiles["stats", b][:, j, :])
 
         def inverse_norm(b):
-            sum_squares = two_graphs.tile([P, TILES], F32, name="sum_squares")
-            nc.vector.tensor_scalar(
-                out=sum_squares[:],
-                in0=tiles["mean_var", b][:, :, 1],
-                scalar1=float(FEATURES),
-                scalar2=TINY,
-                op0=ALU.mult,
-                op1=ALU.max,
-            )
             tiles["inv_norm", b] = two_graphs.tile([P, TILES], F32, name="inv_norm")
-            nc.scalar.activation(out=tiles["inv_norm", b][:], in_=sum_squares[:], func=ACT.Abs_reciprocal_sqrt)
+            nc.scalar.activation(
+                out=tiles["inv_norm", b][:],
+                in_=tiles["mean_var", b][:, :, 1],
+                func=ACT.Abs_reciprocal_sqrt,
+                scale=float(FEATURES),
+                bias=TINY,
+            )
 
         def norm_from_inverse(b):
             tiles["norm", b] = two_graphs.tile([P, TILES], F32, name="norm")

@@ -194,10 +194,14 @@ def tile_pearsonattention_pa_kernel(tc, h, W_h_words, W_h_scales, beta, out):
         def subtract_mean(b, j):
             if j == 0:
                 tiles["x_grouped", b] = two_graphs.tile([P, NODES, PACK], BF16, align_bytes=64, name="x_grouped")
+            run = 4
             nc.vector.tensor_tensor(
-                out=tiles["x_grouped", b][:, block(j), :],
-                in0=tiles["whT", b, j][:].rearrange("p (t r) -> p r t", t=PACK),
-                in1=tiles["mean_rows", b][:, block(j)].unsqueeze(2).to_broadcast([P, P, PACK]),
+                out=tiles["x_grouped", b][:, block(j), :].rearrange("p (c i) t -> p c t i", i=run),
+                in0=tiles["whT", b, j][:].rearrange("p (t c i) -> p c t i", t=PACK, i=run),
+                in1=tiles["mean_rows", b][:, block(j)]
+                .rearrange("p (c i) -> p c i", i=run)
+                .unsqueeze(2)
+                .to_broadcast([P, P // run, PACK, run]),
                 op=ALU.subtract,
             )
 

import concourse.mybir as mybir
from concourse.masks import make_identity

F32 = mybir.dt.float32
BF16 = mybir.dt.bfloat16
I32 = mybir.dt.int32
U32 = mybir.dt.uint32
U8 = mybir.dt.uint8
FP8X4 = mybir.dt.float8_e4m3fn_x4
ACT = mybir.ActivationFunctionType
ALU = mybir.AluOpType

P = 128
PACK = 4
GRAPHS = 4
NODES = 512
FEATURES = 512
TILES = NODES // P
PAIRS = TILES // 2
WORD_HALVES = 2
BANKS = 8
MX_WIDTHS = (128, 256, 512)
EPS = 1e-8
TINY = 1e-30

FLOPS = 2 * GRAPHS * NODES * FEATURES * FEATURES + 2 * GRAPHS * NODES * NODES * FEATURES


def block(i):
    return slice(i * P, (i + 1) * P)


def from_diagonal(i):
    return slice(i * P, NODES)


def tile_pearsonattention_pa_kernel(tc, h, W_h_words, W_h_scales, beta, out):
    nc = tc.nc
    with (
        tc.tile_pool(name="const", bufs=1) as const,
        tc.tile_pool(name="every_graph", bufs=GRAPHS) as every_graph,
        tc.tile_pool(name="two_graphs", bufs=2) as two_graphs,
        tc.tile_pool(name="two_graphs_row_tiles", bufs=2 * TILES) as row_tiles,
        tc.psum_pool(name="psum", bufs=BANKS) as psum,
    ):
        def bank():
            return psum.tile([P, NODES], F32, name="bank")

        tiles = {}

        one = const.tile([P, 1], F32)
        nc.vector.memset(one[:], 1.0)
        table_warm = const.tile([P, 1], F32)
        nc.scalar.activation(out=table_warm[:], in_=one[:], func=ACT.Abs_reciprocal_sqrt)

        identity = const.tile([P, P], F32)
        make_identity(nc, identity[:])

        w_scales = const.tile([P, FEATURES], U8, align_bytes=64)
        nc.vector.memset(w_scales[:].bitcast(I32), 0)

        def load_h(b):
            h_rows = every_graph.tile([P, TILES, FEATURES], BF16, name="h_rows")
            tiles["h_rows", b] = h_rows
            rows = h[b].rearrange("(j p) f -> p j f", p=P)
            for pair in range(PAIRS):
                two = slice(2 * pair, 2 * pair + 2)
                nc.sync.dma_start(out=h_rows[:, two, :], in_=rows[:, two, :])

        load_h(0)
        scale_rows = W_h_scales[0].bitcast(I32)
        for quadrant in range(4):
            nc.sync.dma_start(
                out=w_scales[32 * quadrant : 32 * quadrant + 4, :].bitcast(I32),
                in_=scale_rows[4 * quadrant : 4 * quadrant + 4, :],
            )
        w_codes = const.tile([P, FEATURES], U32, align_bytes=64)
        nc.sync.dma_start(out=w_codes[:].bitcast(I32), in_=W_h_words[0].rearrange("p n t -> p (n t)").bitcast(I32))
        for b in range(1, GRAPHS):
            load_h(b)

        beta_bf16 = const.tile([P, 1], BF16)
        nc.scalar.dma_start(out=beta_bf16[:], in_=beta.partition_broadcast(P))
        beta_f32 = const.tile([P, 1], F32)
        nc.vector.tensor_copy(out=beta_f32[:], in_=beta_bf16[:])

        def transpose_h(b, pair):
            if pair == 0:
                tiles["h_grouped", b] = every_graph.tile([P, NODES, PACK], BF16, align_bytes=64, name="h_grouped")
            hT = bank()[:].rearrange("p (j u r) -> p j u r", j=2, u=WORD_HALVES)
            for jj in range(2):
                words = tiles["h_rows", b][:, 2 * pair + jj, :].bitcast(F32)
                for u in range(WORD_HALVES):
                    nc.tensor.transpose(
                        out=hT[:, jj, u, :], in_=words[:, u : FEATURES // 2 : WORD_HALVES], identity=identity[:]
                    )
            grouped_words = (
                tiles["h_grouped", b][:]
                .rearrange("p r t -> p (r t)")
                .bitcast(F32)
                .rearrange("p (j r u) -> p j r u", j=TILES, u=WORD_HALVES)
            )
            nc.scalar.copy(
                out=grouped_words[:, 2 * pair : 2 * pair + 2, :, :], in_=hT.rearrange("p j u r -> p j r u")
            )

        def quantise(b, grouped, codes, scales, nodes):
            if (codes, b) not in tiles:
                tiles[codes, b] = two_graphs.tile([P, NODES], U32, align_bytes=64, name=codes)
                tiles[scales, b] = two_graphs.tile([P, NODES], U8, align_bytes=64, name=scales)
            nc.vector.quantize_mx(
                out=tiles[codes, b][:, nodes].bitcast(FP8X4),
                scales=tiles[scales, b][:, nodes],
                in_=tiles[grouped, b][:, nodes, :].rearrange("p r t -> p (r t)"),
            )

        def quantise_h(b, pair):
            quantise(b, "h_grouped", "hq_codes", "hq_scales", slice(2 * pair * P, 2 * (pair + 1) * P))

        def quantise_x(b):
            quantise(b, "x_grouped", "xq_codes", "xq_scales", slice(0, NODES))

        def node_statistics(b, j):
            if j == 0:
                tiles["stats", b] = two_graphs.tile([P, TILES, 6], F32, name="stats")
            wh = bank()
            nc.tensor.matmul_mx(
                out=wh[:],
                lhsT=tiles["hq_codes", b][:, block(j)].bitcast(FP8X4),
                lhsT_scale=tiles["hq_scales", b][:, block(j)],
                rhs=w_codes[:].bitcast(FP8X4),
                rhs_scale=w_scales[:],
                start=True,
                stop=True,
            )
            nc.vector.bn_stats(out=tiles["stats", b][:, j, :], in_=wh[:])

        def project_features(b, j):
            whT = bank()
            tiles["whT", b, j] = whT
            for t in range(PACK):
                nc.tensor.matmul_mx(
                    out=whT[:, block(t)],
                    lhsT=w_codes[:, block(t)].bitcast(FP8X4),
                    lhsT_scale=w_scales[:, block(t)],
                    rhs=tiles["hq_codes", b][:, block(j)].bitcast(FP8X4),
                    rhs_scale=tiles["hq_scales", b][:, block(j)],
                    start=True,
                    stop=True,
                )

        def mean_and_variance(b, j):
            if j == 0:
                tiles["mean_var", b] = two_graphs.tile([P, TILES, 2], F32, name="mean_var")
            nc.vector.bn_aggr(out=tiles["mean_var", b][:, j, :], in_=tiles["stats", b][:, j, :])

        def inverse_norm(b):
            tiles["inv_norm", b] = two_graphs.tile([P, TILES], F32, name="inv_norm")
            nc.scalar.activation(
                out=tiles["inv_norm", b][:],
                in_=tiles["mean_var", b][:, :, 1],
                func=ACT.Abs_reciprocal_sqrt,
                scale=float(FEATURES),
                bias=TINY,
            )

        def norm_from_inverse(b):
            tiles["norm", b] = two_graphs.tile([P, TILES], F32, name="norm")
            nc.vector.reciprocal(out=tiles["norm", b][:], in_=tiles["inv_norm", b][:])

        def spread(b, column_of_tile, rows, first, count):
            if (rows, b) not in tiles:
                tiles[rows, b] = two_graphs.tile([P, NODES], F32, name=rows)
            spread_ps = bank()
            for j in range(first, first + count):
                nc.tensor.transpose(
                    out=spread_ps[:, block(j)], in_=column_of_tile(j).to_broadcast([P, P]), identity=identity[:]
                )
            nodes = slice(first * P, (first + count) * P)
            nc.scalar.copy(out=tiles[rows, b][:, nodes], in_=spread_ps[:, nodes])

        def spread_mean(b, pair):
            spread(b, lambda j: tiles["mean_var", b][:, j, 0:1], "mean_rows", 2 * pair, 2)

        def spread_norm(b):
            tiles["norm_rows", b] = bank()
            for j in range(TILES):
                nc.tensor.transpose(
                    out=tiles["norm_rows", b][:, block(j)],
                    in_=tiles["norm", b][:, j : j + 1].to_broadcast([P, P]),
                    identity=identity[:],
                )

        def subtract_mean(b, j):
            if j == 0:
                tiles["x_grouped", b] = two_graphs.tile([P, NODES, PACK], BF16, align_bytes=64, name="x_grouped")
            run = 4
            nc.vector.tensor_tensor(
                out=tiles["x_grouped", b][:, block(j), :].rearrange("p (c i) t -> p c t i", i=run),
                in0=tiles["whT", b, j][:].rearrange("p (t c i) -> p c t i", t=PACK, i=run),
                in1=tiles["mean_rows", b][:, block(j)]
                .rearrange("p (c i) -> p c i", i=run)
                .unsqueeze(2)
                .to_broadcast([P, P // run, PACK, run]),
                op=ALU.subtract,
            )

        def rsqrt_denominator(b, i):
            own = from_diagonal(i)
            tiles["rsqrt_den", b, i] = row_tiles.tile([P, NODES], F32, name="rsqrt_den")
            nc.scalar.activation(
                out=tiles["rsqrt_den", b, i][:, own],
                in_=tiles["norm_rows", b][:, own],
                func=ACT.Abs_reciprocal_sqrt,
                scale=tiles["norm", b][:, i : i + 1],
                bias=EPS,
            )

        def square_denominator(b, i):
            own = from_diagonal(i)
            tiles["inv_den", b, i] = row_tiles.tile([P, NODES], F32, name="inv_den")
            nc.scalar.activation(
                out=tiles["inv_den", b, i][:, own], in_=tiles["rsqrt_den", b, i][:, own], func=ACT.Square
            )

        def inverse_denominators(b, between):
            rsqrt_denominator(b, 0)
            rsqrt_denominator(b, 1)
            for i in range(TILES):
                between(i)
                square_denominator(b, i)
                if i + 2 < TILES:
                    rsqrt_denominator(b, i + 2)

        def covariance(b, i):
            width = min(w for w in MX_WIDTHS if w >= NODES - i * P)
            columns = slice(NODES - width, NODES)
            cov = bank()
            tiles["cov", b, i] = cov
            nc.tensor.matmul_mx(
                out=cov[:, columns],
                lhsT=tiles["xq_codes", b][:, block(i)].bitcast(FP8X4),
                lhsT_scale=tiles["xq_scales", b][:, block(i)],
                rhs=tiles["xq_codes", b][:, columns].bitcast(FP8X4),
                rhs_scale=tiles["xq_scales", b][:, columns],
                start=True,
                stop=True,
            )

        def absolute(b, i):
            own = from_diagonal(i)
            tiles["abs_cov", b, i] = row_tiles.tile([P, NODES], F32, name="abs_cov")
            nc.scalar.activation(out=tiles["abs_cov", b, i][:, own], in_=tiles["cov", b, i][:, own], func=ACT.Abs)

        def scale_own_columns(b, i):
            own = from_diagonal(i)
            tiles["result", b, i] = row_tiles.tile([P, NODES], F32, name="result")
            nc.vector.scalar_tensor_tensor(
                out=tiles["result", b, i][:, own],
                in0=tiles["abs_cov", b, i][:, own],
                scalar=beta_f32[:, 0:1],
                in1=tiles["inv_den", b, i][:, own],
                op0=ALU.mult,
                op1=ALU.mult,
            )

        def mirror(b, i):
            tiles["mirrored", b, i] = bank()
            for j in range(i):
                nc.tensor.transpose(
                    out=tiles["mirrored", b, i][:, block(j)],
                    in_=tiles["result", b, j][:, block(i)],
                    identity=identity[:],
                )

        def complete_and_store(b, i):
            if i > 0:
                nc.scalar.copy(out=tiles["result", b, i][:, 0 : i * P], in_=tiles["mirrored", b, i][:, 0 : i * P])
            nc.sync.dma_start(out=out[b, block(i), :], in_=tiles["result", b, i][:])

        def statistics_of_graph(b, between):
            node_statistics(b, 0)
            node_statistics(b, 1)
            between(0)
            mean_and_variance(b, 0)
            node_statistics(b, 2)
            between(1)
            mean_and_variance(b, 1)
            node_statistics(b, 3)
            mean_and_variance(b, 2)
            mean_and_variance(b, 3)

        for pair in range(PAIRS):
            transpose_h(0, pair)
            quantise_h(0, pair)
        statistics_of_graph(0, lambda k: transpose_h(1, k))
        for j in range(TILES):
            project_features(0, j)
        for pair in range(PAIRS):
            quantise_h(1, pair)
        inverse_norm(0)
        for pair in range(PAIRS):
            spread_mean(0, pair)
        for pair in range(PAIRS):
            transpose_h(2, pair)
        for j in range(TILES):
            subtract_mean(0, j)
        norm_from_inverse(0)
        spread_norm(0)
        inverse_denominators(0, lambda i: None)

        for b in range(GRAPHS):
            nxt = b + 1
            more = nxt < GRAPHS
            quantise_x(b)
            if more:
                statistics_of_graph(nxt, lambda k: covariance(b, k))
            else:
                covariance(b, 0)
                covariance(b, 1)
            absolute(b, 0)
            absolute(b, 1)
            covariance(b, 2)
            covariance(b, 3)
            if more:
                for j in range(TILES):
                    project_features(nxt, j)
            absolute(b, 2)
            absolute(b, 3)
            scale_own_columns(b, 0)
            complete_and_store(b, 0)
            if more:
                inverse_norm(nxt)
                for pair in range(PAIRS):
                    spread_mean(nxt, pair)
            scale_own_columns(b, 1)
            if more:
                norm_from_inverse(nxt)
                spread_norm(nxt)
            scale_own_columns(b, 2)
            if more:
                for j in range(TILES - 1):
                    subtract_mean(nxt, j)
                if nxt + 1 < GRAPHS:
                    for pair in range(PAIRS):
                        quantise_h(nxt + 1, pair)
                subtract_mean(nxt, TILES - 1)
            scale_own_columns(b, 3)
            for i in range(1, TILES):
                mirror(b, i)
            if b + 3 < GRAPHS:
                for pair in range(PAIRS):
                    transpose_h(b + 3, pair)
            if more:
                inverse_denominators(nxt, lambda i: complete_and_store(b, i + 1) if i + 1 < TILES else None)
            else:
                for i in range(1, TILES):
                    complete_and_store(b, i)
